import numpy as np
import ml_dtypes


def mxq(x, axis, fmt="e4m3"):
    dtype, down = {"e4m3": (ml_dtypes.float8_e4m3fn, 7), "e5m2": (ml_dtypes.float8_e5m2, 14)}[fmt]
    v = np.moveaxis(np.asarray(x, np.float32).astype(ml_dtypes.bfloat16).astype(np.float64), axis, -1)
    blocks = v.reshape(v.shape[:-1] + (-1, 32))
    amax = np.abs(blocks).max(-1, keepdims=True)
    byte = np.maximum(np.where(amax > 0, np.frexp(amax)[1] - 1 + 127, 0) - down, 1)
    scale = np.exp2(byte - 127.0)
    codes = (blocks / scale).astype(np.float32).astype(dtype).astype(np.float64)
    return np.moveaxis((codes * scale).reshape(v.shape), -1, axis)


WIDE = False


def mx_kscale(k):
    if not WIDE:
        return np.ones(k)
    levels = np.array([10, -10, 5, -5, 0])
    a = np.random.permutation(np.resize(levels, k // 512 * 4)).reshape(k // 512, 4)
    idx = np.arange(k)
    return np.exp2(a[idx // 512, idx % 128 // 32])


BF16 = ml_dtypes.bfloat16


def bf(x):
    return np.asarray(x, np.float32).astype(BF16)


def f64(x):
    return np.asarray(x).astype(np.float64)


E2M1 = np.array([0.0, 0.5, 1.0, 1.5, 2.0, 3.0, 4.0, 6.0, -0.0, -0.5, -1.0, -1.5, -2.0, -3.0, -4.0, -6.0])


def pack_weight(w, fmt):
    k, n = w.shape
    w = f64(bf(w)).reshape(k // 32, 32, n)
    amax = np.abs(w).max(1)
    if fmt == "e4m3":
        byte = np.frexp(amax)[1] - 1 + 127 - 7
    else:
        mant, ex = np.frexp(amax / 6.0)
        byte = np.where(mant > 0.5, ex, ex - 1) + 127
    byte = np.clip(np.where(amax > 0, byte, 1), 1, 254)
    scaled = (w * np.exp2(127.0 - byte)[:, None, :]).reshape(k, n).astype(np.float32)
    by_word = np.ascontiguousarray(scaled.reshape(k // 512, 128, 4, n).transpose(0, 1, 3, 2))
    if fmt == "e4m3":
        words = by_word.astype(ml_dtypes.float8_e4m3fn).view(np.uint8)
    else:
        c = by_word.astype(ml_dtypes.float4_e2m1fn).view(np.uint8) & 0xF
        words = c[..., 0::2] | (c[..., 1::2] << 4)
    return np.ascontiguousarray(words), np.ascontiguousarray(byte.astype(np.uint8).reshape(k // 512, 16, n))


def unpack_weight(words, scales, fmt):
    g, p, n, _ = words.shape
    if fmt == "e4m3":
        vals = np.ascontiguousarray(words).view(ml_dtypes.float8_e4m3fn).astype(np.float64)
    else:
        nib = np.empty((g, p, n, 4), np.uint8)
        nib[..., 0::2] = words & 0xF
        nib[..., 1::2] = words >> 4
        vals = E2M1[nib]
    vals = vals * np.repeat(np.exp2(scales.astype(np.float64) - 127.0), 8, axis=1)[..., None]
    return vals.transpose(0, 1, 3, 2).reshape(g * 512, n)


B, T, D, F, LNS = 64, 40, 512, 2048, 8


def erf(z):
    a = np.minimum(np.abs(z), 6.0)
    d = 2.0 * a * a
    term = a.copy()
    total = a.copy()
    n = 0
    while np.any(term > 1e-18 * total):
        n += 1
        term = term * d / (2 * n + 1)
        total = total + term
    return np.sign(z) * np.minimum(2.0 / np.sqrt(np.pi) * np.exp(-a * a) * total, 1.0)


def gelu(v):
    return 0.5 * v * (1.0 + erf(v / np.sqrt(2.0)))


def setup_inputs():
    s = mx_kscale(D)
    x_tail = bf(np.random.standard_normal((B, LNS, D)) * s)
    w1 = np.random.standard_normal((LNS, D, F)) / np.sqrt(D) / s[None, :, None]
    w2 = np.random.standard_normal((LNS, F, D)) / np.sqrt(F)
    w1_words, w1_scales = pack_weight(w1.reshape(-1, F), "e4m3")
    w2_words, w2_scales = pack_weight(w2.reshape(-1, D), "e4m3")
    return {"x_tail": x_tail,
            "W1NS_words": w1_words, "W1NS_scales": w1_scales,
            "W2NS_words": w2_words, "W2NS_scales": w2_scales}


def reference(x_tail, W1NS_words, W1NS_scales, W2NS_words, W2NS_scales):
    xp = f64(x_tail).transpose(1, 0, 2)
    h = gelu(mxq(xp, 2, "e4m3") @ unpack_weight(W1NS_words, W1NS_scales, "e4m3").reshape(LNS, D, F))
    y = mxq(h, 2, "e4m3") @ unpack_weight(W2NS_words, W2NS_scales, "e4m3").reshape(LNS, F, D)
    return y.transpose(1, 0, 2)

@@ -1,0 +1,152 @@
+from contextlib import ExitStack
+
+import concourse.mybir as mybir
+from concourse.masks import make_identity
+
+F32 = mybir.dt.float32
+BF16 = mybir.dt.bfloat16
+I32 = mybir.dt.int32
+U32 = mybir.dt.uint32
+U8 = mybir.dt.uint8
+FP8X4 = mybir.dt.float8_e4m3fn_x4
+GELU = mybir.ActivationFunctionType.Gelu
+
+P = 128
+PACK = 4
+K_PASS = P * PACK
+N_PASS = 512
+
+B, T, D, F = 64, 8, 512, 2048
+PAIRS = T // 2
+F_GROUPS = F // K_PASS
+QUADRANTS = 4
+PLANES = 4
+
+FLOPS = 2 * T * B * D * F * 2
+
+
+def load_packed_planes(nc, planes, scales):
+    for quadrant in range(QUADRANTS):
+        nc.sync.dma_start(
+            out=planes[32 * quadrant : 32 * quadrant + 4 * PLANES, :].bitcast(I32),
+            in_=scales[:, 4 * quadrant : 4 * quadrant + 4, :].bitcast(I32),
+        )
+
+
+def tile_mixedffn_pa_e_kernel(tc, x_tail, W1NS_words, W1NS_scales, W2NS_words, W2NS_scales, out):
+    nc = tc.nc
+    with ExitStack() as stack:
+        keep = stack.enter_context(tc.tile_pool(name="keep", bufs=1))
+        work = stack.enter_context(tc.tile_pool(name="work", bufs=2))
+        psum_h = stack.enter_context(tc.psum_pool(name="psum_h", bufs=4))
+        psum_t = stack.enter_context(tc.psum_pool(name="psum_t", bufs=2))
+        psum_o = stack.enter_context(tc.psum_pool(name="psum_o", bufs=2))
+
+        w1_planes = keep.tile([P, T // PLANES, F], U8, align_bytes=64)
+        w2_planes = keep.tile([P, T, D], U8, align_bytes=64)
+        nc.vector.memset(w1_planes[:].bitcast(I32), 0)
+        nc.vector.memset(w2_planes[:].bitcast(I32), 0)
+
+        x_sb = keep.tile([P, PAIRS, D], BF16)
+        x_by_parity = x_tail.rearrange("b (q s) d -> s b q d", s=2)
+        for s in range(2):
+            nc.scalar.dma_start(out=x_sb[B * s : B * (s + 1), :, :], in_=x_by_parity[s])
+
+        w1_words = []
+        for t in range(T):
+            words = keep.tile([P, F], U32, name="w1_words%d" % t, align_bytes=64)
+            nc.sync.dma_start(out=words[:].bitcast(I32), in_=W1NS_words[t].rearrange("p n j -> p (n j)").bitcast(I32))
+            w1_words.append(words)
+            if t < T // PLANES:
+                load_packed_planes(nc, w1_planes[:, t, :], W1NS_scales[PLANES * t : PLANES * (t + 1)])
+        w2_words = []
+        for t in range(T):
+            groups = slice(F_GROUPS * t, F_GROUPS * (t + 1))
+            load_packed_planes(nc, w2_planes[:, t, :], W2NS_scales[groups])
+            words = keep.tile([P, F_GROUPS, D], U32, name="w2_words%d" % t, align_bytes=64)
+            nc.sync.dma_start(
+                out=words[:].bitcast(I32), in_=W2NS_words[groups].rearrange("g p n j -> p g (n j)").bitcast(I32)
+            )
+            w2_words.append(words)
+
+        ident_f32 = keep.tile([P, P], F32)
+        make_identity(nc, ident_f32[:])
+        ident_bf16 = keep.tile([P, P], BF16)
+        make_identity(nc, ident_bf16[:])
+
+        x_words = x_sb[:].bitcast(F32)
+        x_grouped = keep.tile([P, PAIRS, P, PACK], BF16, align_bytes=64)
+        x_grouped_words = x_grouped[:].bitcast(F32)
+        x_codes = keep.tile([P, PAIRS, P], U32, align_bytes=64)
+        x_scales = keep.tile([P, PAIRS, P], U8, align_bytes=64)
+        for half in range(2):
+            pairs = slice(2 * half, 2 * half + 2)
+            xT = psum_t.tile([P, 2, 2, P], F32, tag="transposed")
+            for i in range(2):
+                for u in range(2):
+                    nc.tensor.transpose(xT[:, i, u, :], x_words[:, 2 * half + i, u : D // 2 : 2], ident_f32[:])
+            nc.vector.tensor_copy(out=x_grouped_words[:, pairs, :, :], in_=xT[:].rearrange("p i u c -> p i c u"))
+            nc.vector.quantize_mx(
+                out=x_codes[:, pairs, :].rearrange("p i c -> p (i c)").bitcast(FP8X4),
+                scales=x_scales[:, pairs, :].rearrange("p i c -> p (i c)"),
+                in_=x_grouped[:, pairs, :, :].rearrange("p i c j -> p (i c j)"),
+            )
+
+        h_codes = []
+        h_scales = []
+        for q in range(PAIRS):
+            h_sb = work.tile([P, F_GROUPS, PACK, P], BF16)
+            for s in range(2):
+                t = 2 * q + s
+                rows = slice(B * s, B * (s + 1))
+                for g in range(F_GROUPS):
+                    cols = slice(N_PASS * g, N_PASS * (g + 1))
+                    acc = psum_h.tile([P, N_PASS], F32)
+                    nc.tensor.matmul_mx(
+                        out=acc[:],
+                        lhsT=x_codes[:, q, :].bitcast(FP8X4),
+                        lhsT_scale=x_scales[:, q, :],
+                        rhs=w1_words[t][:, cols].bitcast(FP8X4),
+                        rhs_scale=w1_planes[4 * (t % PLANES) : P, t // PLANES, cols],
+                        start=True,
+                        stop=True,
+                    )
+                    nc.scalar.activation(
+                        out=h_sb[rows, g, :, :], in_=acc[rows, :].rearrange("b (p j) -> b j p", j=PACK), func=GELU
+                    )
+
+            h_grouped = work.tile([P, F_GROUPS, P, PACK], BF16, align_bytes=64)
+            codes = keep.tile([P, F_GROUPS, P], U32, name="h_codes%d" % q, align_bytes=64)
+            scales = keep.tile([P, F_GROUPS, P], U8, name="h_scales%d" % q, align_bytes=64)
+            for half in range(2):
+                groups = slice(2 * half, 2 * half + 2)
+                hT = psum_t.tile([P, 2, PACK, P], BF16, tag="transposed")
+                for i in range(2):
+                    for j in range(PACK):
+                        nc.tensor.transpose(hT[:, i, j, :], h_sb[:, 2 * half + i, j, :], ident_bf16[:])
+                nc.vector.tensor_copy(out=h_grouped[:, groups, :, :], in_=hT[:].rearrange("p i j c -> p i c j"))
+                nc.vector.quantize_mx(
+                    out=codes[:, groups, :].rearrange("p i c -> p (i c)").bitcast(FP8X4),
+                    scales=scales[:, groups, :].rearrange("p i c -> p (i c)"),
+                    in_=h_grouped[:, groups, :, :].rearrange("p i c j -> p (i c j)"),
+                )
+            h_codes.append(codes)
+            h_scales.append(scales)
+
+        for t in range(T):
+            q, s = divmod(t, 2)
+            rows = slice(B * s, B * (s + 1))
+            acc = psum_o.tile([P, D], F32)
+            for g in range(F_GROUPS):
+                nc.tensor.matmul_mx(
+                    out=acc[:],
+                    lhsT=h_codes[q][:, g, :].bitcast(FP8X4),
+                    lhsT_scale=h_scales[q][:, g, :],
+                    rhs=w2_words[t][:, g, :].bitcast(FP8X4),
+                    rhs_scale=w2_planes[4 * g : P, t, :],
+                    start=(g == 0),
+                    stop=(g == F_GROUPS - 1),
+                )
+            result = work.tile([P, D], F32)
+            nc.vector.tensor_copy(out=result[rows, :], in_=acc[rows, :])
+            nc.scalar.dma_start(out=out[:, t, :], in_=result[rows, :])

@@ -62,7 +62,6 @@ def tile_mixedffn_pa_e_kernel(tc, x_tail, W1NS_words, W1NS_scales, W2NS_words, W
         w2_words = []
         for t in range(T):
             groups = slice(F_GROUPS * t, F_GROUPS * (t + 1))
-            load_packed_planes(nc, w2_planes[:, t, :], W2NS_scales[groups])
             words = keep.tile([P, F_GROUPS, D], U32, name="w2_words%d" % t, align_bytes=64)
             nc.sync.dma_start(
                 out=words[:].bitcast(I32), in_=W2NS_words[groups].rearrange("g p n j -> p g (n j)").bitcast(I32)
@@ -73,6 +72,13 @@ def tile_mixedffn_pa_e_kernel(tc, x_tail, W1NS_words, W1NS_scales, W2NS_words, W
         make_identity(nc, ident_f32[:])
         ident_bf16 = keep.tile([P, P], BF16)
         make_identity(nc, ident_bf16[:])
+
+        w2_scales_by_row = W2NS_scales.rearrange("(t g) (quadrant r) n -> g r quadrant t n", g=F_GROUPS, r=4)
+        for g in range(F_GROUPS):
+            for r in range(4):
+                nc.gpsimd.dma_start(
+                    out=w2_planes[4 * g + r : P : 32, :, :].bitcast(F32), in_=w2_scales_by_row[g, r].bitcast(F32)
+                )
 
         x_words = x_sb[:].bitcast(F32)
         x_grouped = keep.tile([P, PAIRS, P, PACK], BF16, align_bytes=64)

@@ -62,6 +62,7 @@ def tile_mixedffn_pa_e_kernel(tc, x_tail, W1NS_words, W1NS_scales, W2NS_words, W
         w2_words = []
         for t in range(T):
             groups = slice(F_GROUPS * t, F_GROUPS * (t + 1))
+            load_packed_planes(nc, w2_planes[:, t, :], W2NS_scales[groups])
             words = keep.tile([P, F_GROUPS, D], U32, name="w2_words%d" % t, align_bytes=64)
             nc.sync.dma_start(
                 out=words[:].bitcast(I32), in_=W2NS_words[groups].rearrange("g p n j -> p g (n j)").bitcast(I32)
@@ -72,13 +73,6 @@ def tile_mixedffn_pa_e_kernel(tc, x_tail, W1NS_words, W1NS_scales, W2NS_words, W
         make_identity(nc, ident_f32[:])
         ident_bf16 = keep.tile([P, P], BF16)
         make_identity(nc, ident_bf16[:])
-
-        w2_scales_by_row = W2NS_scales.rearrange("(t g) (quadrant r) n -> g r quadrant t n", g=F_GROUPS, r=4)
-        for g in range(F_GROUPS):
-            for r in range(4):
-                nc.gpsimd.dma_start(
-                    out=w2_planes[4 * g + r : P : 32, :, :].bitcast(F32), in_=w2_scales_by_row[g, r].bitcast(F32)
-                )
 
         x_words = x_sb[:].bitcast(F32)
         x_grouped = keep.tile([P, PAIRS, P, PACK], BF16, align_bytes=64)
@@ -153,6 +147,6 @@ def tile_mixedffn_pa_e_kernel(tc, x_tail, W1NS_words, W1NS_scales, W2NS_words, W
                     start=(g == 0),
                     stop=(g == F_GROUPS - 1),
                 )
-            result = work.tile([P, D], F32)
+            result = keep.tile([P, D], F32, name="result%d" % t)
             nc.vector.tensor_copy(out=result[rows, :], in_=acc[rows, :])
             nc.scalar.dma_start(out=out[:, t, :], in_=result[rows, :])

@@ -50,7 +50,7 @@ def tile_mixedffn_pa_e_kernel(tc, x_tail, W1NS_words, W1NS_scales, W2NS_words, W
         x_sb = keep.tile([P, PAIRS, D], BF16)
         x_by_parity = x_tail.rearrange("b (q s) d -> s b q d", s=2)
         for s in range(2):
-            nc.scalar.dma_start(out=x_sb[B * s : B * (s + 1), :, :], in_=x_by_parity[s])
+            nc.sync.dma_start(out=x_sb[s : P : 2, :, :], in_=x_by_parity[s])
 
         w1_words = []
         for t in range(T):
@@ -62,7 +62,6 @@ def tile_mixedffn_pa_e_kernel(tc, x_tail, W1NS_words, W1NS_scales, W2NS_words, W
         w2_words = []
         for t in range(T):
             groups = slice(F_GROUPS * t, F_GROUPS * (t + 1))
-            load_packed_planes(nc, w2_planes[:, t, :], W2NS_scales[groups])
             words = keep.tile([P, F_GROUPS, D], U32, name="w2_words%d" % t, align_bytes=64)
             nc.sync.dma_start(
                 out=words[:].bitcast(I32), in_=W2NS_words[groups].rearrange("g p n j -> p g (n j)").bitcast(I32)
@@ -73,6 +72,13 @@ def tile_mixedffn_pa_e_kernel(tc, x_tail, W1NS_words, W1NS_scales, W2NS_words, W
         make_identity(nc, ident_f32[:])
         ident_bf16 = keep.tile([P, P], BF16)
         make_identity(nc, ident_bf16[:])
+
+        w2_scales_by_row = W2NS_scales.rearrange("(t g) (quadrant r) n -> g r quadrant t n", g=F_GROUPS, r=4)
+        for g in range(F_GROUPS):
+            for r in range(4):
+                nc.gpsimd.dma_start(
+                    out=w2_planes[4 * g + r : P : 32, :, :].bitcast(F32), in_=w2_scales_by_row[g, r].bitcast(F32)
+                )
 
         x_words = x_sb[:].bitcast(F32)
         x_grouped = keep.tile([P, PAIRS, P, PACK], BF16, align_bytes=64)
@@ -85,7 +91,11 @@ def tile_mixedffn_pa_e_kernel(tc, x_tail, W1NS_words, W1NS_scales, W2NS_words, W
             for i in range(2):
                 for u in range(2):
                     nc.tensor.transpose(xT[:, i, u, :], x_words[:, 2 * half + i, u : D // 2 : 2], ident_f32[:])
-            nc.vector.tensor_copy(out=x_grouped_words[:, pairs, :, :], in_=xT[:].rearrange("p i u c -> p i c u"))
+            for i in range(2):
+                nc.vector.tensor_copy(
+                    out=x_grouped_words[:, 2 * half + i, :, :].rearrange("p (s b) u -> p s b u", s=2),
+                    in_=xT[:, i, :, :].rearrange("p u (b s) -> p s b u", s=2),
+                )
             nc.vector.quantize_mx(
                 out=x_codes[:, pairs, :].rearrange("p i c -> p (i c)").bitcast(FP8X4),
                 scales=x_scales[:, pairs, :].rearrange("p i c -> p (i c)"),
@@ -124,7 +134,11 @@ def tile_mixedffn_pa_e_kernel(tc, x_tail, W1NS_words, W1NS_scales, W2NS_words, W
                 for i in range(2):
                     for j in range(PACK):
                         nc.tensor.transpose(hT[:, i, j, :], h_sb[:, 2 * half + i, j, :], ident_bf16[:])
-                nc.vector.tensor_copy(out=h_grouped[:, groups, :, :], in_=hT[:].rearrange("p i j c -> p i c j"))
+                for i in range(2):
+                    nc.vector.tensor_copy(
+                        out=h_grouped[:, 2 * half + i, :, :].rearrange("p (b s) j -> p b s j", s=2),
+                        in_=hT[:, i, :, :].rearrange("p j (s b) -> p b s j", s=2),
+                    )
                 nc.vector.quantize_mx(
                     out=codes[:, groups, :].rearrange("p i c -> p (i c)").bitcast(FP8X4),
                     scales=scales[:, groups, :].rearrange("p i c -> p (i c)"),
@@ -135,7 +149,6 @@ def tile_mixedffn_pa_e_kernel(tc, x_tail, W1NS_words, W1NS_scales, W2NS_words, W
 
         for t in range(T):
             q, s = divmod(t, 2)
-            rows = slice(B * s, B * (s + 1))
             acc = psum_o.tile([P, D], F32)
             for g in range(F_GROUPS):
                 nc.tensor.matmul_mx(
@@ -148,5 +161,5 @@ def tile_mixedffn_pa_e_kernel(tc, x_tail, W1NS_words, W1NS_scales, W2NS_words, W
                     stop=(g == F_GROUPS - 1),
                 )
             result = keep.tile([P, D], F32, name="result%d" % t)
-            nc.vector.tensor_copy(out=result[rows, :], in_=acc[rows, :])
-            nc.scalar.dma_start(out=out[:, t, :], in_=result[rows, :])
+            nc.vector.tensor_copy(out=result[:], in_=acc[:])
+            nc.scalar.dma_start(out=out[:, t, :], in_=result[s : P : 2, :])

@@ -63,9 +63,11 @@ def tile_mixedffn_pa_e_kernel(tc, x_tail, W1NS_words, W1NS_scales, W2NS_words, W
         for t in range(T):
             groups = slice(F_GROUPS * t, F_GROUPS * (t + 1))
             words = keep.tile([P, F_GROUPS, D], U32, name="w2_words%d" % t, align_bytes=64)
-            nc.sync.dma_start(
-                out=words[:].bitcast(I32), in_=W2NS_words[groups].rearrange("g p n j -> p g (n j)").bitcast(I32)
-            )
+            source = W2NS_words[groups].rearrange("g p n j -> p g (n j)").bitcast(I32)
+            groups_per_dma = 1 if t == T - 1 else F_GROUPS
+            for g in range(0, F_GROUPS, groups_per_dma):
+                part = slice(g, g + groups_per_dma)
+                nc.sync.dma_start(out=words[:, part, :].bitcast(I32), in_=source[:, part, :])
             w2_words.append(words)
 
         ident_f32 = keep.tile([P, P], F32)

@@ -75,11 +75,13 @@ def tile_mixedffn_pa_e_kernel(tc, x_tail, W1NS_words, W1NS_scales, W2NS_words, W
         ident_bf16 = keep.tile([P, P], BF16)
         make_identity(nc, ident_bf16[:])
 
-        w2_scales_by_row = W2NS_scales.rearrange("(t g) (quadrant r) n -> g r quadrant t n", g=F_GROUPS, r=4)
-        for g in range(F_GROUPS):
+        w2_scales_by_row = W2NS_scales.rearrange("(t g) (quadrant r) n -> quadrant r g t n", g=F_GROUPS, r=4)
+        for quadrant in range(QUADRANTS):
             for r in range(4):
+                first = 32 * quadrant + r
                 nc.gpsimd.dma_start(
-                    out=w2_planes[4 * g + r : P : 32, :, :].bitcast(F32), in_=w2_scales_by_row[g, r].bitcast(F32)
+                    out=w2_planes[first : first + 4 * PLANES : 4, :, :].bitcast(F32),
+                    in_=w2_scales_by_row[quadrant, r].bitcast(F32),
                 )
 
         x_words = x_sb[:].bitcast(F32)

@@ -27,9 +27,9 @@ FLOPS = 2 * T * B * D * F * 2
 
 def load_packed_planes(nc, planes, scales):
     for quadrant in range(QUADRANTS):
-        nc.sync.dma_start(
-            out=planes[32 * quadrant : 32 * quadrant + 4 * PLANES, :].bitcast(I32),
-            in_=scales[:, 4 * quadrant : 4 * quadrant + 4, :].bitcast(I32),
+        nc.gpsimd.dma_start(
+            out=planes[32 * quadrant : 32 * quadrant + 4 * PLANES, :].bitcast(F32),
+            in_=scales[:, 4 * quadrant : 4 * quadrant + 4, :].bitcast(F32),
         )
 
 
@@ -57,8 +57,6 @@ def tile_mixedffn_pa_e_kernel(tc, x_tail, W1NS_words, W1NS_scales, W2NS_words, W
             words = keep.tile([P, F], U32, name="w1_words%d" % t, align_bytes=64)
             nc.sync.dma_start(out=words[:].bitcast(I32), in_=W1NS_words[t].rearrange("p n j -> p (n j)").bitcast(I32))
             w1_words.append(words)
-            if t < T // PLANES:
-                load_packed_planes(nc, w1_planes[:, t, :], W1NS_scales[PLANES * t : PLANES * (t + 1)])
         w2_words = []
         for t in range(T):
             groups = slice(F_GROUPS * t, F_GROUPS * (t + 1))
@@ -72,8 +70,10 @@ def tile_mixedffn_pa_e_kernel(tc, x_tail, W1NS_words, W1NS_scales, W2NS_words, W
 
         ident_f32 = keep.tile([P, P], F32)
         make_identity(nc, ident_f32[:])
+        load_packed_planes(nc, w1_planes[:, 0, :], W1NS_scales[0:PLANES])
         ident_bf16 = keep.tile([P, P], BF16)
         make_identity(nc, ident_bf16[:])
+        load_packed_planes(nc, w1_planes[:, 1, :], W1NS_scales[PLANES : 2 * PLANES])
 
         w2_scales_by_row = W2NS_scales.rearrange("(t g) (quadrant r) n -> quadrant r g t n", g=F_GROUPS, r=4)
         for quadrant in range(QUADRANTS):

@@ -166,4 +166,4 @@ def tile_mixedffn_pa_e_kernel(tc, x_tail, W1NS_words, W1NS_scales, W2NS_words, W
                 )
             result = keep.tile([P, D], F32, name="result%d" % t)
             nc.vector.tensor_copy(out=result[:], in_=acc[:])
-            nc.scalar.dma_start(out=out[:, t, :], in_=result[s : P : 2, :])
+            nc.sync.dma_start(out=out[:, t, :], in_=result[s : P : 2, :])

@@ -22,6 +22,8 @@ F_GROUPS = F // K_PASS
 QUADRANTS = 4
 PLANES = 4
 
+LAST_COLUMNS = [slice(0, D // 2), slice(D // 2, D)]
+
 FLOPS = 2 * T * B * D * F * 2
 
 
@@ -65,7 +67,8 @@ def tile_mixedffn_pa_e_kernel(tc, x_tail, W1NS_words, W1NS_scales, W2NS_words, W
             groups_per_dma = 1 if t == T - 1 else F_GROUPS
             for g in range(0, F_GROUPS, groups_per_dma):
                 part = slice(g, g + groups_per_dma)
-                nc.sync.dma_start(out=words[:, part, :].bitcast(I32), in_=source[:, part, :])
+                for cols in LAST_COLUMNS if (t == T - 1 and g == F_GROUPS - 1) else [slice(0, D)]:
+                    nc.sync.dma_start(out=words[:, part, cols].bitcast(I32), in_=source[:, part, cols])
             w2_words.append(words)
 
         ident_f32 = keep.tile([P, P], F32)
@@ -153,17 +156,23 @@ def tile_mixedffn_pa_e_kernel(tc, x_tail, W1NS_words, W1NS_scales, W2NS_words, W
 
         for t in range(T):
             q, s = divmod(t, 2)
-            acc = psum_o.tile([P, D], F32)
+            column_parts = LAST_COLUMNS if t == T - 1 else [slice(0, D)]
+            accs = []
+            for i in range(len(column_parts)):
+                acc = psum_o.tile([P, D // len(column_parts)], F32)
+                accs.append(acc)
             for g in range(F_GROUPS):
-                nc.tensor.matmul_mx(
-                    out=acc[:],
-                    lhsT=h_codes[q][:, g, :].bitcast(FP8X4),
-                    lhsT_scale=h_scales[q][:, g, :],
-                    rhs=w2_words[t][:, g, :].bitcast(FP8X4),
-                    rhs_scale=w2_planes[4 * g : P, t, :],
-                    start=(g == 0),
-                    stop=(g == F_GROUPS - 1),
-                )
+                for acc, cols in zip(accs, column_parts):
+                    nc.tensor.matmul_mx(
+                        out=acc[:],
+                        lhsT=h_codes[q][:, g, :].bitcast(FP8X4),
+                        lhsT_scale=h_scales[q][:, g, :],
+                        rhs=w2_words[t][:, g, cols].bitcast(FP8X4),
+                        rhs_scale=w2_planes[4 * g : P, t, cols],
+                        start=(g == 0),
+                        stop=(g == F_GROUPS - 1),
+                    )
             result = keep.tile([P, D], F32, name="result%d" % t)
-            nc.vector.tensor_copy(out=result[:], in_=acc[:])
-            nc.sync.dma_start(out=out[:, t, :], in_=result[s : P : 2, :])
+            for acc, cols in zip(accs, column_parts):
+                nc.vector.tensor_copy(out=result[:, cols], in_=acc[:])
+                nc.sync.dma_start(out=out[:, t, cols], in_=result[s : P : 2, cols])

@@ -175,4 +175,4 @@ def tile_mixedffn_pa_e_kernel(tc, x_tail, W1NS_words, W1NS_scales, W2NS_words, W
             result = keep.tile([P, D], F32, name="result%d" % t)
             for acc, cols in zip(accs, column_parts):
                 nc.vector.tensor_copy(out=result[:, cols], in_=acc[:])
-                nc.sync.dma_start(out=out[:, t, cols], in_=result[s : P : 2, cols])
+            nc.sync.dma_start(out=out[:, t, :], in_=result[s : P : 2, :])

from contextlib import ExitStack

import concourse.mybir as mybir
from concourse.masks import make_identity

F32 = mybir.dt.float32
BF16 = mybir.dt.bfloat16
I32 = mybir.dt.int32
U32 = mybir.dt.uint32
U8 = mybir.dt.uint8
FP8X4 = mybir.dt.float8_e4m3fn_x4
GELU = mybir.ActivationFunctionType.Gelu

P = 128
PACK = 4
K_PASS = P * PACK
N_PASS = 512

B, T, D, F = 64, 8, 512, 2048
PAIRS = T // 2
F_GROUPS = F // K_PASS
QUADRANTS = 4
PLANES = 4

LAST_COLUMNS = [slice(0, D // 2), slice(D // 2, D)]

FLOPS = 2 * T * B * D * F * 2


def load_packed_planes(nc, planes, scales):
    for quadrant in range(QUADRANTS):
        nc.gpsimd.dma_start(
            out=planes[32 * quadrant : 32 * quadrant + 4 * PLANES, :].bitcast(F32),
            in_=scales[:, 4 * quadrant : 4 * quadrant + 4, :].bitcast(F32),
        )


def tile_mixedffn_pa_e_kernel(tc, x_tail, W1NS_words, W1NS_scales, W2NS_words, W2NS_scales, out):
    nc = tc.nc
    with ExitStack() as stack:
        keep = stack.enter_context(tc.tile_pool(name="keep", bufs=1))
        work = stack.enter_context(tc.tile_pool(name="work", bufs=2))
        psum_h = stack.enter_context(tc.psum_pool(name="psum_h", bufs=4))
        psum_t = stack.enter_context(tc.psum_pool(name="psum_t", bufs=2))
        psum_o = stack.enter_context(tc.psum_pool(name="psum_o", bufs=2))

        w1_planes = keep.tile([P, T // PLANES, F], U8, align_bytes=64)
        w2_planes = keep.tile([P, T, D], U8, align_bytes=64)
        nc.vector.memset(w1_planes[:].bitcast(I32), 0)
        nc.vector.memset(w2_planes[:].bitcast(I32), 0)

        x_sb = keep.tile([P, PAIRS, D], BF16)
        x_by_parity = x_tail.rearrange("b (q s) d -> s b q d", s=2)
        for s in range(2):
            nc.sync.dma_start(out=x_sb[s : P : 2, :, :], in_=x_by_parity[s])

        w1_words = []
        for t in range(T):
            words = keep.tile([P, F], U32, name="w1_words%d" % t, align_bytes=64)
            nc.sync.dma_start(out=words[:].bitcast(I32), in_=W1NS_words[t].rearrange("p n j -> p (n j)").bitcast(I32))
            w1_words.append(words)
        w2_words = []
        for t in range(T):
            groups = slice(F_GROUPS * t, F_GROUPS * (t + 1))
            words = keep.tile([P, F_GROUPS, D], U32, name="w2_words%d" % t, align_bytes=64)
            source = W2NS_words[groups].rearrange("g p n j -> p g (n j)").bitcast(I32)
            groups_per_dma = 1 if t == T - 1 else F_GROUPS
            for g in range(0, F_GROUPS, groups_per_dma):
                part = slice(g, g + groups_per_dma)
                for cols in LAST_COLUMNS if (t == T - 1 and g == F_GROUPS - 1) else [slice(0, D)]:
                    nc.sync.dma_start(out=words[:, part, cols].bitcast(I32), in_=source[:, part, cols])
            w2_words.append(words)

        ident_f32 = keep.tile([P, P], F32)
        make_identity(nc, ident_f32[:])
        load_packed_planes(nc, w1_planes[:, 0, :], W1NS_scales[0:PLANES])
        ident_bf16 = keep.tile([P, P], BF16)
        make_identity(nc, ident_bf16[:])
        load_packed_planes(nc, w1_planes[:, 1, :], W1NS_scales[PLANES : 2 * PLANES])

        w2_scales_by_row = W2NS_scales.rearrange("(t g) (quadrant r) n -> quadrant r g t n", g=F_GROUPS, r=4)
        for quadrant in range(QUADRANTS):
            for r in range(4):
                first = 32 * quadrant + r
                nc.gpsimd.dma_start(
                    out=w2_planes[first : first + 4 * PLANES : 4, :, :].bitcast(F32),
                    in_=w2_scales_by_row[quadrant, r].bitcast(F32),
                )

        x_words = x_sb[:].bitcast(F32)
        x_grouped = keep.tile([P, PAIRS, P, PACK], BF16, align_bytes=64)
        x_grouped_words = x_grouped[:].bitcast(F32)
        x_codes = keep.tile([P, PAIRS, P], U32, align_bytes=64)
        x_scales = keep.tile([P, PAIRS, P], U8, align_bytes=64)
        for half in range(2):
            pairs = slice(2 * half, 2 * half + 2)
            xT = psum_t.tile([P, 2, 2, P], F32, tag="transposed")
            for i in range(2):
                for u in range(2):
                    nc.tensor.transpose(xT[:, i, u, :], x_words[:, 2 * half + i, u : D // 2 : 2], ident_f32[:])
            for i in range(2):
                nc.vector.tensor_copy(
                    out=x_grouped_words[:, 2 * half + i, :, :].rearrange("p (s b) u -> p s b u", s=2),
                    in_=xT[:, i, :, :].rearrange("p u (b s) -> p s b u", s=2),
                )
            nc.vector.quantize_mx(
                out=x_codes[:, pairs, :].rearrange("p i c -> p (i c)").bitcast(FP8X4),
                scales=x_scales[:, pairs, :].rearrange("p i c -> p (i c)"),
                in_=x_grouped[:, pairs, :, :].rearrange("p i c j -> p (i c j)"),
            )

        h_codes = []
        h_scales = []
        for q in range(PAIRS):
            h_sb = work.tile([P, F_GROUPS, PACK, P], BF16)
            for s in range(2):
                t = 2 * q + s
                rows = slice(B * s, B * (s + 1))
                for g in range(F_GROUPS):
                    cols = slice(N_PASS * g, N_PASS * (g + 1))
                    acc = psum_h.tile([P, N_PASS], F32)
                    nc.tensor.matmul_mx(
                        out=acc[:],
                        lhsT=x_codes[:, q, :].bitcast(FP8X4),
                        lhsT_scale=x_scales[:, q, :],
                        rhs=w1_words[t][:, cols].bitcast(FP8X4),
                        rhs_scale=w1_planes[4 * (t % PLANES) : P, t // PLANES, cols],
                        start=True,
                        stop=True,
                    )
                    nc.scalar.activation(
                        out=h_sb[rows, g, :, :], in_=acc[rows, :].rearrange("b (p j) -> b j p", j=PACK), func=GELU
                    )

            h_grouped = work.tile([P, F_GROUPS, P, PACK], BF16, align_bytes=64)
            codes = keep.tile([P, F_GROUPS, P], U32, name="h_codes%d" % q, align_bytes=64)
            scales = keep.tile([P, F_GROUPS, P], U8, name="h_scales%d" % q, align_bytes=64)
            for half in range(2):
                groups = slice(2 * half, 2 * half + 2)
                hT = psum_t.tile([P, 2, PACK, P], BF16, tag="transposed")
                for i in range(2):
                    for j in range(PACK):
                        nc.tensor.transpose(hT[:, i, j, :], h_sb[:, 2 * half + i, j, :], ident_bf16[:])
                for i in range(2):
                    nc.vector.tensor_copy(
                        out=h_grouped[:, 2 * half + i, :, :].rearrange("p (b s) j -> p b s j", s=2),
                        in_=hT[:, i, :, :].rearrange("p j (s b) -> p b s j", s=2),
                    )
                nc.vector.quantize_mx(
                    out=codes[:, groups, :].rearrange("p i c -> p (i c)").bitcast(FP8X4),
                    scales=scales[:, groups, :].rearrange("p i c -> p (i c)"),
                    in_=h_grouped[:, groups, :, :].rearrange("p i c j -> p (i c j)"),
                )
            h_codes.append(codes)
            h_scales.append(scales)

        for t in range(T):
            q, s = divmod(t, 2)
            column_parts = LAST_COLUMNS if t == T - 1 else [slice(0, D)]
            accs = []
            for i in range(len(column_parts)):
                acc = psum_o.tile([P, D // len(column_parts)], F32)
                accs.append(acc)
            for g in range(F_GROUPS):
                for acc, cols in zip(accs, column_parts):
                    nc.tensor.matmul_mx(
                        out=acc[:],
                        lhsT=h_codes[q][:, g, :].bitcast(FP8X4),
                        lhsT_scale=h_scales[q][:, g, :],
                        rhs=w2_words[t][:, g, cols].bitcast(FP8X4),
                        rhs_scale=w2_planes[4 * g : P, t, cols],
                        start=(g == 0),
                        stop=(g == F_GROUPS - 1),
                    )
            result = keep.tile([P, D], F32, name="result%d" % t)
            for acc, cols in zip(accs, column_parts):
                nc.vector.tensor_copy(out=result[:, cols], in_=acc[:])
            nc.sync.dma_start(out=out[:, t, :], in_=result[s : P : 2, :])
